import numpy as np
import ml_dtypes


def mxq(x, axis, fmt="e4m3"):
    dtype, down = {"e4m3": (ml_dtypes.float8_e4m3fn, 7), "e5m2": (ml_dtypes.float8_e5m2, 14)}[fmt]
    v = np.moveaxis(np.asarray(x, np.float32).astype(ml_dtypes.bfloat16).astype(np.float64), axis, -1)
    blocks = v.reshape(v.shape[:-1] + (-1, 32))
    amax = np.abs(blocks).max(-1, keepdims=True)
    byte = np.maximum(np.where(amax > 0, np.frexp(amax)[1] - 1 + 127, 0) - down, 1)
    scale = np.exp2(byte - 127.0)
    codes = (blocks / scale).astype(np.float32).astype(dtype).astype(np.float64)
    return np.moveaxis((codes * scale).reshape(v.shape), -1, axis)


WIDE = False


def mx_kscale(k):
    if not WIDE:
        return np.ones(k)
    levels = np.array([10, -10, 5, -5, 0])
    if k % 512:
        return np.exp2(np.random.permutation(np.resize(levels, k // 32))).repeat(32)
    a = np.empty((k // 512, 16))
    for p in range(k // 512):
        a[p, :8] = np.random.permutation(np.resize(levels, 8))
        for g in range(8):
            far = levels[np.abs(levels - a[p, g]) >= 10]
            a[p, g + 8] = far[np.random.randint(len(far))]
    return np.exp2(a.ravel()).repeat(32)


BF16 = ml_dtypes.bfloat16


def bf(x):
    return np.asarray(x, np.float32).astype(BF16)


def f64(x):
    return np.asarray(x).astype(np.float64)


B, IN_C, OUT_C, H, W, K, STRIDE, PAD = 32, 512, 128, 2, 2, 3, 1, 1
OH = (H + 2 * PAD - K) // STRIDE + 1
OW = (W + 2 * PAD - K) // STRIDE + 1


def _span(t, n_in, n_out):
    lo = max(0, -((t - PAD) // STRIDE))
    hi = min(n_out, (n_in - 1 + PAD - t) // STRIDE + 1)
    return lo, hi


def setup_inputs():
    s = mx_kscale(IN_C)
    x = np.random.standard_normal((B, IN_C, H, W)) * s[None, :, None, None]
    weights = np.random.uniform(0.0, 1.0, (OH, OW, OUT_C, IN_C, K, K)) * (1.7 / np.sqrt(IN_C * K * K)) / s[None, None, None, :, None, None]
    bias = np.random.uniform(0.0, 1.0, (OUT_C, OH, OW))
    return {"x": bf(x), "weights": bf(weights), "bias": bf(bias)}


def reference(x, weights, bias):
    xq = mxq(f64(x), 1, "e4m3")
    wf = f64(weights)
    acc = np.zeros((OH, OW, B, OUT_C))
    for i in range(K):
        h0, h1 = _span(i, H, OH)
        for j in range(K):
            w0, w1 = _span(j, W, OW)
            xs = xq[:, :, h0 * STRIDE + i - PAD:(h1 - 1) * STRIDE + i - PAD + 1:STRIDE,
                    w0 * STRIDE + j - PAD:(w1 - 1) * STRIDE + j - PAD + 1:STRIDE]
            wq = mxq(wf[h0:h1, w0:w1, :, :, i, j], 3, "e4m3")
            acc[h0:h1, w0:w1] += xs.transpose(2, 3, 0, 1) @ wq.transpose(0, 1, 3, 2)
    return acc.transpose(2, 3, 0, 1) + f64(bias)[None]

@@ -1,0 +1,183 @@
+from contextlib import ExitStack
+
+import concourse.mybir as mybir
+from concourse.masks import make_identity
+
+BF16 = mybir.dt.bfloat16
+F32 = mybir.dt.float32
+U32 = mybir.dt.uint32
+U8 = mybir.dt.uint8
+FP8X4 = mybir.dt.float8_e4m3fn_x4
+
+P = 128
+PACK = 4
+PAIR = 2
+WORDS = PACK // PAIR
+BATCH = 32
+CHANNELS = 512
+OUT_CH = 128
+SIDE = 2
+TAPS = 3
+PIXELS = SIDE * SIDE
+LOCATIONS = SIDE * SIDE
+QUARTERS = 4
+C_QUARTER = CHANNELS // QUARTERS
+QUARTERS_PER_LOAD = 2
+LOADS_PER_LOCATION = QUARTERS // QUARTERS_PER_LOAD
+LOADS = LOCATIONS * LOADS_PER_LOCATION
+STEPS = LOCATIONS * QUARTERS
+X_STRIDE = 64
+X_SLOTS = QUARTERS + 1
+C_VECTOR = 13 * C_QUARTER // 16
+
+FLOPS = 2 * BATCH * OUT_CH * LOCATIONS * PIXELS * CHANNELS
+BYTES = (
+    2 * BATCH * CHANNELS * PIXELS
+    + 2 * LOCATIONS * OUT_CH * CHANNELS * PIXELS
+    + 2 * OUT_CH * LOCATIONS
+    + 4 * BATCH * OUT_CH * LOCATIONS
+)
+
+
+def tile_locallyconnected2d_s_kernel(tc, x, weights, bias, out):
+    nc = tc.nc
+    with ExitStack() as stack:
+        keep = stack.enter_context(tc.tile_pool(name="keep", bufs=1))
+        w_pool = stack.enter_context(tc.tile_pool(name="w_pool", bufs=LOADS))
+        stage = stack.enter_context(tc.tile_pool(name="stage", bufs=4))
+        psum_t = stack.enter_context(tc.psum_pool(name="psum_t", bufs=4))
+        psum_x = stack.enter_context(tc.psum_pool(name="psum_x", bufs=1))
+        psum_acc = stack.enter_context(tc.psum_pool(name="psum_acc", bufs=1))
+
+        x_raw = keep.tile([P, C_QUARTER, PIXELS], BF16)
+        nc.sync.dma_start(
+            out=x_raw[:], in_=x.rearrange("b (k c) y z -> (b k) c (y z)", k=QUARTERS)
+        )
+        bias_rows = keep.tile([BATCH, OUT_CH, LOCATIONS], BF16)
+        nc.scalar.dma_start(
+            out=bias_rows[:].rearrange("b o l -> b (o l)"),
+            in_=bias.rearrange("o h w -> (o h w)").partition_broadcast(BATCH),
+        )
+        w_rows = weights.rearrange("h w o (u c) i j -> (h w) u o c i j", u=LOADS_PER_LOCATION)
+        w_raw = []
+        for n in range(LOADS):
+            w_tile = w_pool.tile([P, QUARTERS_PER_LOAD * C_QUARTER, TAPS, TAPS], BF16, name="w_tile")
+            loc, u = divmod(n, LOADS_PER_LOCATION)
+            nc.sync.dma_start(out=w_tile[:], in_=w_rows[loc, u])
+            w_raw.append(w_tile)
+
+        identity = keep.tile([P, P], F32)
+        make_identity(nc, identity[:])
+
+        x_sorted = keep.tile([P, PIXELS, C_QUARTER], BF16)
+        x_t = psum_x.tile([P, WORDS, P], F32)
+        x_grouped = keep.tile([P, X_SLOTS, X_STRIDE, PACK], BF16, align_bytes=64)
+        x_codes = keep.tile([P, X_SLOTS * X_STRIDE], U32, align_bytes=64)
+        x_scales = keep.tile([P, X_SLOTS * X_STRIDE], U8, align_bytes=64)
+
+        nc.vector.memset(x_grouped[:].bitcast(F32), 0.0)
+
+        def transpose_words(out, in_, s):
+            words = in_.rearrange("p q c -> p (q c)").bitcast(F32)
+            nc.tensor.transpose(out, words[:, s::WORDS], identity[:])
+
+        def sort_x():
+            nc.vector.tensor_copy(out=x_sorted[:], in_=x_raw[:].rearrange("p c q -> p q c"))
+
+        def transpose_x():
+            for s in range(WORDS):
+                transpose_words(x_t[:, s, :], x_sorted[:], s)
+
+        def regroup_x():
+            nc.scalar.copy(
+                out=x_grouped[:, :QUARTERS, :BATCH, :].bitcast(F32),
+                in_=x_t[:].rearrange("p s (b k) -> p k b s", k=QUARTERS),
+            )
+
+        def quantise_x():
+            values = x_grouped[:].rearrange("p k m t -> p (k m t)")
+            split = QUARTERS * X_STRIDE
+            for cols in (slice(0, split), slice(split, split + X_STRIDE)):
+                nc.vector.quantize_mx(
+                    out=x_codes[:, cols].bitcast(FP8X4),
+                    scales=x_scales[:, cols],
+                    in_=values[:, cols.start * PACK : cols.stop * PACK],
+                )
+
+        w_codes = keep.tile([P, STEPS, OUT_CH], U32, align_bytes=64)
+        w_scales = keep.tile([P, STEPS, OUT_CH], U8, align_bytes=64)
+        acc = psum_acc.tile([P, LOCATIONS, OUT_CH], F32)
+        w_sorted = {}
+        w_t = {}
+        w_grouped = {}
+
+        def sort_taps(step):
+            n, part = divmod(step, QUARTERS_PER_LOAD)
+            h, w = divmod(step // QUARTERS, SIDE)
+            taps = w_raw[n][
+                :,
+                part * C_QUARTER : (part + 1) * C_QUARTER,
+                1 - h : 1 - h + SIDE,
+                1 - w : 1 - w + SIDE,
+            ]
+            w_sorted[step] = stage.tile([P, PIXELS, C_QUARTER], BF16, name="w_sorted")
+            by_channel = w_sorted[step][:].rearrange("p (y z) c -> p c y z", y=SIDE)
+            nc.vector.tensor_copy(out=by_channel[:, :C_VECTOR], in_=taps[:, :C_VECTOR])
+            nc.scalar.copy(out=by_channel[:, C_VECTOR:], in_=taps[:, C_VECTOR:])
+
+        def transpose_taps(step):
+            w_t[step] = psum_t.tile([P, WORDS, P], F32, name="w_t")
+            for s in range(WORDS):
+                transpose_words(w_t[step][:, s, :], w_sorted[step][:], s)
+
+        def regroup(step):
+            w_grouped[step] = stage.tile([P, OUT_CH, PACK], BF16, align_bytes=64, name="w_grouped")
+            nc.scalar.copy(
+                out=w_grouped[step][:].bitcast(F32),
+                in_=w_t[step][:].rearrange("p s o -> p o s"),
+            )
+
+        def quantise(step):
+            nc.vector.quantize_mx(
+                out=w_codes[:, step, :].bitcast(FP8X4),
+                scales=w_scales[:, step, :],
+                in_=w_grouped[step][:].rearrange("p o t -> p (o t)"),
+            )
+
+        def multiply(step):
+            loc, k = divmod(step, QUARTERS)
+            x_cols = slice(k * X_STRIDE, k * X_STRIDE + P)
+            nc.tensor.matmul_mx(
+                out=acc[:, loc, :],
+                lhsT=x_codes[:, x_cols].bitcast(FP8X4),
+                lhsT_scale=x_scales[:, x_cols],
+                rhs=w_codes[:, step, :].bitcast(FP8X4),
+                rhs_scale=w_scales[:, step, :],
+                start=(k == 0),
+                stop=(k == QUARTERS - 1),
+            )
+
+        sort_x()
+        transpose_x()
+        regroup_x()
+        quantise_x()
+        for step in range(STEPS):
+            sort_taps(step)
+            transpose_taps(step)
+            regroup(step)
+            quantise(step)
+            if step % QUARTERS == QUARTERS - 1:
+                for done in range(step - QUARTERS + 1, step + 1):
+                    multiply(done)
+
+        result = keep.tile([BATCH, OUT_CH, LOCATIONS], F32)
+        nc.vector.tensor_tensor(
+            out=result[:],
+            in0=acc[0:BATCH].rearrange("b l o -> b o l"),
+            in1=bias_rows[:],
+            op=mybir.AluOpType.add,
+        )
+        nc.sync.dma_start(
+            out=out.rearrange("b o h w -> b (o h w)"),
+            in_=result[:].rearrange("b o l -> b (o l)"),
+        )

@@ -54,10 +54,6 @@ def tile_locallyconnected2d_s_kernel(tc, x, weights, bias, out):
             out=x_raw[:], in_=x.rearrange("b (k c) y z -> (b k) c (y z)", k=QUARTERS)
         )
         bias_rows = keep.tile([BATCH, OUT_CH, LOCATIONS], BF16)
-        nc.scalar.dma_start(
-            out=bias_rows[:].rearrange("b o l -> b (o l)"),
-            in_=bias.rearrange("o h w -> (o h w)").partition_broadcast(BATCH),
-        )
         w_rows = weights.rearrange("h w o (u c) i j -> (h w) u o c i j", u=LOADS_PER_LOCATION)
         w_raw = []
         for n in range(LOADS):
@@ -65,6 +61,10 @@ def tile_locallyconnected2d_s_kernel(tc, x, weights, bias, out):
             loc, u = divmod(n, LOADS_PER_LOCATION)
             nc.sync.dma_start(out=w_tile[:], in_=w_rows[loc, u])
             w_raw.append(w_tile)
+        nc.sync.dma_start(
+            out=bias_rows[:].rearrange("b o l -> b (o l)"),
+            in_=bias.rearrange("o h w -> (o h w)").partition_broadcast(BATCH),
+        )
 
         identity = keep.tile([P, P], F32)
         make_identity(nc, identity[:])

@@ -22,13 +22,12 @@ PIXELS = SIDE * SIDE
 LOCATIONS = SIDE * SIDE
 QUARTERS = 4
 C_QUARTER = CHANNELS // QUARTERS
-QUARTERS_PER_LOAD = 2
-LOADS_PER_LOCATION = QUARTERS // QUARTERS_PER_LOAD
-LOADS = LOCATIONS * LOADS_PER_LOCATION
 STEPS = LOCATIONS * QUARTERS
+STEPS_PER_LOAD = (1, 1) + (2,) * (STEPS // 2 - 2) + (1, 1)
 X_STRIDE = 64
 X_SLOTS = QUARTERS + 1
-C_VECTOR = 13 * C_QUARTER // 16
+QUANTISE_LAG = 2
+MULTIPLY_LAG = 4
 
 FLOPS = 2 * BATCH * OUT_CH * LOCATIONS * PIXELS * CHANNELS
 BYTES = (
@@ -43,7 +42,7 @@ def tile_locallyconnected2d_s_kernel(tc, x, weights, bias, out):
     nc = tc.nc
     with ExitStack() as stack:
         keep = stack.enter_context(tc.tile_pool(name="keep", bufs=1))
-        w_pool = stack.enter_context(tc.tile_pool(name="w_pool", bufs=LOADS))
+        w_pool = stack.enter_context(tc.tile_pool(name="w_pool", bufs=len(STEPS_PER_LOAD)))
         stage = stack.enter_context(tc.tile_pool(name="stage", bufs=4))
         psum_t = stack.enter_context(tc.psum_pool(name="psum_t", bufs=4))
         psum_x = stack.enter_context(tc.psum_pool(name="psum_x", bufs=1))
@@ -54,13 +53,15 @@ def tile_locallyconnected2d_s_kernel(tc, x, weights, bias, out):
             out=x_raw[:], in_=x.rearrange("b (k c) y z -> (b k) c (y z)", k=QUARTERS)
         )
         bias_rows = keep.tile([BATCH, OUT_CH, LOCATIONS], BF16)
-        w_rows = weights.rearrange("h w o (u c) i j -> (h w) u o c i j", u=LOADS_PER_LOCATION)
+        w_rows = weights.rearrange("h w o c i j -> (h w) o c i j")
         w_raw = []
-        for n in range(LOADS):
-            w_tile = w_pool.tile([P, QUARTERS_PER_LOAD * C_QUARTER, TAPS, TAPS], BF16, name="w_tile")
-            loc, u = divmod(n, LOADS_PER_LOCATION)
-            nc.sync.dma_start(out=w_tile[:], in_=w_rows[loc, u])
-            w_raw.append(w_tile)
+        for steps in STEPS_PER_LOAD:
+            loc, k = divmod(len(w_raw), QUARTERS)
+            w_tile = w_pool.tile([P, steps * C_QUARTER, TAPS, TAPS], BF16, name="w_tile")
+            nc.sync.dma_start(
+                out=w_tile[:], in_=w_rows[loc, :, k * C_QUARTER : (k + steps) * C_QUARTER]
+            )
+            w_raw.extend(w_tile[:, n * C_QUARTER : (n + 1) * C_QUARTER] for n in range(steps))
         nc.sync.dma_start(
             out=bias_rows[:].rearrange("b o l -> b (o l)"),
             in_=bias.rearrange("o h w -> (o h w)").partition_broadcast(BATCH),
@@ -112,18 +113,11 @@ def tile_locallyconnected2d_s_kernel(tc, x, weights, bias, out):
         w_grouped = {}
 
         def sort_taps(step):
-            n, part = divmod(step, QUARTERS_PER_LOAD)
             h, w = divmod(step // QUARTERS, SIDE)
-            taps = w_raw[n][
-                :,
-                part * C_QUARTER : (part + 1) * C_QUARTER,
-                1 - h : 1 - h + SIDE,
-                1 - w : 1 - w + SIDE,
-            ]
+            taps = w_raw[step][:, :, 1 - h : 1 - h + SIDE, 1 - w : 1 - w + SIDE]
             w_sorted[step] = stage.tile([P, PIXELS, C_QUARTER], BF16, name="w_sorted")
             by_channel = w_sorted[step][:].rearrange("p (y z) c -> p c y z", y=SIDE)
-            nc.vector.tensor_copy(out=by_channel[:, :C_VECTOR], in_=taps[:, :C_VECTOR])
-            nc.scalar.copy(out=by_channel[:, C_VECTOR:], in_=taps[:, C_VECTOR:])
+            nc.vector.tensor_copy(out=by_channel, in_=taps)
 
         def transpose_taps(step):
             w_t[step] = psum_t.tile([P, WORDS, P], F32, name="w_t")
@@ -157,18 +151,21 @@ def tile_locallyconnected2d_s_kernel(tc, x, weights, bias, out):
                 stop=(k == QUARTERS - 1),
             )
 
-        sort_x()
-        transpose_x()
-        regroup_x()
-        quantise_x()
-        for step in range(STEPS):
-            sort_taps(step)
-            transpose_taps(step)
-            regroup(step)
-            quantise(step)
-            if step % QUARTERS == QUARTERS - 1:
-                for done in range(step - QUARTERS + 1, step + 1):
-                    multiply(done)
+        with tc.manual_schedule():
+            sort_x()
+            transpose_x()
+            regroup_x()
+            for i in range(STEPS + MULTIPLY_LAG):
+                if i < STEPS:
+                    sort_taps(i)
+                    transpose_taps(i)
+                    regroup(i)
+                if i == 1:
+                    quantise_x()
+                if 0 <= i - QUANTISE_LAG < STEPS:
+                    quantise(i - QUANTISE_LAG)
+                if i >= MULTIPLY_LAG:
+                    multiply(i - MULTIPLY_LAG)
 
         result = keep.tile([BATCH, OUT_CH, LOCATIONS], F32)
         nc.vector.tensor_tensor(

@@ -21,13 +21,14 @@ TAPS = 3
 PIXELS = SIDE * SIDE
 LOCATIONS = SIDE * SIDE
 QUARTERS = 4
+P_PIXEL = P // PIXELS
 C_QUARTER = CHANNELS // QUARTERS
 STEPS = LOCATIONS * QUARTERS
-STEPS_PER_LOAD = (1, 1) + (2,) * (STEPS // 2 - 2) + (1, 1)
+GROUPS = (1, 1) + (2,) * (STEPS // 2 - 2) + (1, 1)
 X_STRIDE = 64
 X_SLOTS = QUARTERS + 1
-QUANTISE_LAG = 2
-MULTIPLY_LAG = 4
+QUANTISE_LAG = 1
+MULTIPLY_LAG = 2
 
 FLOPS = 2 * BATCH * OUT_CH * LOCATIONS * PIXELS * CHANNELS
 BYTES = (
@@ -42,7 +43,7 @@ def tile_locallyconnected2d_s_kernel(tc, x, weights, bias, out):
     nc = tc.nc
     with ExitStack() as stack:
         keep = stack.enter_context(tc.tile_pool(name="keep", bufs=1))
-        w_pool = stack.enter_context(tc.tile_pool(name="w_pool", bufs=len(STEPS_PER_LOAD)))
+        w_pool = stack.enter_context(tc.tile_pool(name="w_pool", bufs=len(GROUPS)))
         stage = stack.enter_context(tc.tile_pool(name="stage", bufs=4))
         psum_t = stack.enter_context(tc.psum_pool(name="psum_t", bufs=4))
         psum_x = stack.enter_context(tc.psum_pool(name="psum_x", bufs=1))
@@ -55,13 +56,15 @@ def tile_locallyconnected2d_s_kernel(tc, x, weights, bias, out):
         bias_rows = keep.tile([BATCH, OUT_CH, LOCATIONS], BF16)
         w_rows = weights.rearrange("h w o c i j -> (h w) o c i j")
         w_raw = []
-        for steps in STEPS_PER_LOAD:
-            loc, k = divmod(len(w_raw), QUARTERS)
+        first_step = []
+        for steps in GROUPS:
+            first_step.append(sum(GROUPS[: len(w_raw)]))
+            loc, k = divmod(first_step[-1], QUARTERS)
             w_tile = w_pool.tile([P, steps * C_QUARTER, TAPS, TAPS], BF16, name="w_tile")
             nc.sync.dma_start(
                 out=w_tile[:], in_=w_rows[loc, :, k * C_QUARTER : (k + steps) * C_QUARTER]
             )
-            w_raw.extend(w_tile[:, n * C_QUARTER : (n + 1) * C_QUARTER] for n in range(steps))
+            w_raw.append(w_tile)
         nc.sync.dma_start(
             out=bias_rows[:].rearrange("b o l -> b (o l)"),
             in_=bias.rearrange("o h w -> (o h w)").partition_broadcast(BATCH),
@@ -70,7 +73,7 @@ def tile_locallyconnected2d_s_kernel(tc, x, weights, bias, out):
         identity = keep.tile([P, P], F32)
         make_identity(nc, identity[:])
 
-        x_sorted = keep.tile([P, PIXELS, C_QUARTER], BF16)
+        x_sorted = keep.tile([P, WORDS, PIXELS, P_PIXEL, PAIR], BF16)
         x_t = psum_x.tile([P, WORDS, P], F32)
         x_grouped = keep.tile([P, X_SLOTS, X_STRIDE, PACK], BF16, align_bytes=64)
         x_codes = keep.tile([P, X_SLOTS * X_STRIDE], U32, align_bytes=64)
@@ -78,16 +81,19 @@ def tile_locallyconnected2d_s_kernel(tc, x, weights, bias, out):
 
         nc.vector.memset(x_grouped[:].bitcast(F32), 0.0)
 
-        def transpose_words(out, in_, s):
-            words = in_.rearrange("p q c -> p (q c)").bitcast(F32)
-            nc.tensor.transpose(out, words[:, s::WORDS], identity[:])
-
         def sort_x():
-            nc.vector.tensor_copy(out=x_sorted[:], in_=x_raw[:].rearrange("p c q -> p q c"))
+            by_s = x_raw[:].rearrange("r (p s e) q -> r s p e q", s=WORDS, e=PAIR)
+            for s in range(WORDS):
+                nc.vector.tensor_copy(
+                    out=x_sorted[:, s].rearrange("r q p e -> r p e q"), in_=by_s[:, s]
+                )
+
+        def transpose_words(out, in_):
+            nc.tensor.transpose(out, in_.rearrange("r q p e -> r (q p e)").bitcast(F32), identity[:])
 
         def transpose_x():
             for s in range(WORDS):
-                transpose_words(x_t[:, s, :], x_sorted[:], s)
+                transpose_words(x_t[:, s, :], x_sorted[:, s])
 
         def regroup_x():
             nc.scalar.copy(
@@ -112,57 +118,61 @@ def tile_locallyconnected2d_s_kernel(tc, x, weights, bias, out):
         w_t = {}
         w_grouped = {}
 
-        def sort_taps(step):
-            h, w = divmod(step // QUARTERS, SIDE)
-            taps = w_raw[step][:, :, 1 - h : 1 - h + SIDE, 1 - w : 1 - w + SIDE]
-            w_sorted[step] = stage.tile([P, PIXELS, C_QUARTER], BF16, name="w_sorted")
-            by_channel = w_sorted[step][:].rearrange("p (y z) c -> p c y z", y=SIDE)
-            nc.vector.tensor_copy(out=by_channel, in_=taps)
-
-        def transpose_taps(step):
-            w_t[step] = psum_t.tile([P, WORDS, P], F32, name="w_t")
+        def sort_taps(g):
+            h, w = divmod(first_step[g] // QUARTERS, SIDE)
+            taps = w_raw[g][:, :, 1 - h : 1 - h + SIDE, 1 - w : 1 - w + SIDE]
+            by_s = taps.rearrange("o (n p s e) y z -> o s n p e y z", p=P_PIXEL, s=WORDS, e=PAIR)
+            w_sorted[g] = stage.tile([P, GROUPS[g], WORDS, PIXELS, P_PIXEL, PAIR], BF16, name="w_sorted")
+            by_channel = w_sorted[g][:].rearrange("o n s (y z) p e -> o s n p e y z", y=SIDE)
             for s in range(WORDS):
-                transpose_words(w_t[step][:, s, :], w_sorted[step][:], s)
+                nc.vector.tensor_copy(out=by_channel[:, s], in_=by_s[:, s])
 
-        def regroup(step):
-            w_grouped[step] = stage.tile([P, OUT_CH, PACK], BF16, align_bytes=64, name="w_grouped")
+        def transpose_taps(g):
+            w_t[g] = psum_t.tile([P, GROUPS[g], WORDS, P], F32, name="w_t")
+            for s in range(WORDS):
+                for n in range(GROUPS[g]):
+                    transpose_words(w_t[g][:, n, s, :], w_sorted[g][:, n, s])
+
+        def regroup(g):
+            w_grouped[g] = stage.tile([P, GROUPS[g], OUT_CH, PACK], BF16, align_bytes=64, name="w_grouped")
             nc.scalar.copy(
-                out=w_grouped[step][:].bitcast(F32),
-                in_=w_t[step][:].rearrange("p s o -> p o s"),
+                out=w_grouped[g][:].bitcast(F32), in_=w_t[g][:].rearrange("p n s o -> p n o s")
             )
 
-        def quantise(step):
+        def quantise(g):
+            steps = slice(first_step[g], first_step[g] + GROUPS[g])
             nc.vector.quantize_mx(
-                out=w_codes[:, step, :].bitcast(FP8X4),
-                scales=w_scales[:, step, :],
-                in_=w_grouped[step][:].rearrange("p o t -> p (o t)"),
+                out=w_codes[:, steps, :].rearrange("p n o -> p (n o)").bitcast(FP8X4),
+                scales=w_scales[:, steps, :].rearrange("p n o -> p (n o)"),
+                in_=w_grouped[g][:].rearrange("p n o t -> p (n o t)"),
             )
 
-        def multiply(step):
-            loc, k = divmod(step, QUARTERS)
-            x_cols = slice(k * X_STRIDE, k * X_STRIDE + P)
-            nc.tensor.matmul_mx(
-                out=acc[:, loc, :],
-                lhsT=x_codes[:, x_cols].bitcast(FP8X4),
-                lhsT_scale=x_scales[:, x_cols],
-                rhs=w_codes[:, step, :].bitcast(FP8X4),
-                rhs_scale=w_scales[:, step, :],
-                start=(k == 0),
-                stop=(k == QUARTERS - 1),
-            )
+        def multiply(g):
+            for step in range(first_step[g], first_step[g] + GROUPS[g]):
+                loc, k = divmod(step, QUARTERS)
+                x_cols = slice(k * X_STRIDE, k * X_STRIDE + P)
+                nc.tensor.matmul_mx(
+                    out=acc[:, loc, :],
+                    lhsT=x_codes[:, x_cols].bitcast(FP8X4),
+                    lhsT_scale=x_scales[:, x_cols],
+                    rhs=w_codes[:, step, :].bitcast(FP8X4),
+                    rhs_scale=w_scales[:, step, :],
+                    start=(k == 0),
+                    stop=(k == QUARTERS - 1),
+                )
 
         with tc.manual_schedule():
             sort_x()
             transpose_x()
             regroup_x()
-            for i in range(STEPS + MULTIPLY_LAG):
-                if i < STEPS:
+            for i in range(len(GROUPS) + MULTIPLY_LAG):
+                if i < len(GROUPS):
                     sort_taps(i)
                     transpose_taps(i)
                     regroup(i)
                 if i == 1:
                     quantise_x()
-                if 0 <= i - QUANTISE_LAG < STEPS:
+                if 0 <= i - QUANTISE_LAG < len(GROUPS):
                     quantise(i - QUANTISE_LAG)
                 if i >= MULTIPLY_LAG:
                     multiply(i - MULTIPLY_LAG)

@@ -27,8 +27,8 @@ STEPS = LOCATIONS * QUARTERS
 GROUPS = (1, 1) + (2,) * (STEPS // 2 - 2) + (1, 1)
 X_STRIDE = 64
 X_SLOTS = QUARTERS + 1
-QUANTISE_LAG = 1
-MULTIPLY_LAG = 2
+QUANTISE_LAG = 2
+MULTIPLY_LAG = 3
 
 FLOPS = 2 * BATCH * OUT_CH * LOCATIONS * PIXELS * CHANNELS
 BYTES = (

@@ -147,9 +147,9 @@ def tile_locallyconnected2d_s_kernel(tc, x, weights, bias, out):
                 in_=w_grouped[g][:].rearrange("p n o t -> p (n o t)"),
             )
 
-        def multiply(g):
-            for step in range(first_step[g], first_step[g] + GROUPS[g]):
-                loc, k = divmod(step, QUARTERS)
+        def multiply(loc):
+            for k in range(QUARTERS):
+                step = loc * QUARTERS + k
                 x_cols = slice(k * X_STRIDE, k * X_STRIDE + P)
                 nc.tensor.matmul_mx(
                     out=acc[:, loc, :],
@@ -175,7 +175,9 @@ def tile_locallyconnected2d_s_kernel(tc, x, weights, bias, out):
                 if 0 <= i - QUANTISE_LAG < len(GROUPS):
                     quantise(i - QUANTISE_LAG)
                 if i >= MULTIPLY_LAG:
-                    multiply(i - MULTIPLY_LAG)
+                    loc, k = divmod(first_step[i - MULTIPLY_LAG] + GROUPS[i - MULTIPLY_LAG], QUARTERS)
+                    if k == 0:
+                        multiply(loc - 1)
 
         result = keep.tile([BATCH, OUT_CH, LOCATIONS], F32)
         nc.vector.tensor_tensor(

@@ -42,14 +42,14 @@ BYTES = (
 def tile_locallyconnected2d_s_kernel(tc, x, weights, bias, out):
     nc = tc.nc
     with ExitStack() as stack:
-        keep = stack.enter_context(tc.tile_pool(name="keep", bufs=1))
         w_pool = stack.enter_context(tc.tile_pool(name="w_pool", bufs=len(GROUPS)))
+        keep = stack.enter_context(tc.tile_pool(name="keep", bufs=1))
         stage = stack.enter_context(tc.tile_pool(name="stage", bufs=4))
         psum_t = stack.enter_context(tc.psum_pool(name="psum_t", bufs=4))
         psum_x = stack.enter_context(tc.psum_pool(name="psum_x", bufs=1))
         psum_acc = stack.enter_context(tc.psum_pool(name="psum_acc", bufs=1))
 
-        x_raw = keep.tile([P, C_QUARTER, PIXELS], BF16)
+        x_raw = keep.tile([P, C_QUARTER, PIXELS], BF16, align_bytes=256)
         nc.sync.dma_start(
             out=x_raw[:], in_=x.rearrange("b (k c) y z -> (b k) c (y z)", k=QUARTERS)
         )
@@ -60,7 +60,7 @@ def tile_locallyconnected2d_s_kernel(tc, x, weights, bias, out):
         for steps in GROUPS:
             first_step.append(sum(GROUPS[: len(w_raw)]))
             loc, k = divmod(first_step[-1], QUARTERS)
-            w_tile = w_pool.tile([P, steps * C_QUARTER, TAPS, TAPS], BF16, name="w_tile")
+            w_tile = w_pool.tile([P, steps * C_QUARTER, TAPS, TAPS], BF16, align_bytes=256, name="w_tile")
             nc.sync.dma_start(
                 out=w_tile[:], in_=w_rows[loc, :, k * C_QUARTER : (k + steps) * C_QUARTER]
             )

@@ -24,7 +24,7 @@ QUARTERS = 4
 P_PIXEL = P // PIXELS
 C_QUARTER = CHANNELS // QUARTERS
 STEPS = LOCATIONS * QUARTERS
-GROUPS = (1, 1) + (2,) * (STEPS // 2 - 2) + (1, 1)
+GROUPS = (2,) * (STEPS // 2 - 1) + (1, 1)
 X_STRIDE = 64
 X_SLOTS = QUARTERS + 1
 QUANTISE_LAG = 2
@@ -133,19 +133,27 @@ def tile_locallyconnected2d_s_kernel(tc, x, weights, bias, out):
                 for n in range(GROUPS[g]):
                     transpose_words(w_t[g][:, n, s, :], w_sorted[g][:, n, s])
 
+        def o_parts(g):
+            parts = 2 if g == len(GROUPS) - 1 else 1
+            width = OUT_CH // parts
+            return [slice(n * width, (n + 1) * width) for n in range(parts)]
+
         def regroup(g):
             w_grouped[g] = stage.tile([P, GROUPS[g], OUT_CH, PACK], BF16, align_bytes=64, name="w_grouped")
-            nc.scalar.copy(
-                out=w_grouped[g][:].bitcast(F32), in_=w_t[g][:].rearrange("p n s o -> p n o s")
-            )
+            for o_range in o_parts(g):
+                nc.scalar.copy(
+                    out=w_grouped[g][:, :, o_range].bitcast(F32),
+                    in_=w_t[g][:, :, :, o_range].rearrange("p n s o -> p n o s"),
+                )
 
         def quantise(g):
             steps = slice(first_step[g], first_step[g] + GROUPS[g])
-            nc.vector.quantize_mx(
-                out=w_codes[:, steps, :].rearrange("p n o -> p (n o)").bitcast(FP8X4),
-                scales=w_scales[:, steps, :].rearrange("p n o -> p (n o)"),
-                in_=w_grouped[g][:].rearrange("p n o t -> p (n o t)"),
-            )
+            for o_range in o_parts(g):
+                nc.vector.quantize_mx(
+                    out=w_codes[:, steps, o_range].rearrange("p n o -> p (n o)").bitcast(FP8X4),
+                    scales=w_scales[:, steps, o_range].rearrange("p n o -> p (n o)"),
+                    in_=w_grouped[g][:, :, o_range].rearrange("p n o t -> p (n o t)"),
+                )
 
         def multiply(loc):
             for k in range(QUARTERS):
@@ -170,7 +178,7 @@ def tile_locallyconnected2d_s_kernel(tc, x, weights, bias, out):
                     sort_taps(i)
                     transpose_taps(i)
                     regroup(i)
-                if i == 1:
+                if i == 0:
                     quantise_x()
                 if 0 <= i - QUANTISE_LAG < len(GROUPS):
                     quantise(i - QUANTISE_LAG)

@@ -26,7 +26,9 @@ C_QUARTER = CHANNELS // QUARTERS
 STEPS = LOCATIONS * QUARTERS
 GROUPS = (2,) * (STEPS // 2 - 1) + (1, 1)
 X_STRIDE = 64
-X_SLOTS = QUARTERS + 1
+X_COLS = QUARTERS * X_STRIDE
+ZERO_COLS = 256
+TAIL = len(GROUPS) - 2
 QUANTISE_LAG = 2
 MULTIPLY_LAG = 3
 
@@ -48,6 +50,7 @@ def tile_locallyconnected2d_s_kernel(tc, x, weights, bias, out):
         psum_t = stack.enter_context(tc.psum_pool(name="psum_t", bufs=4))
         psum_x = stack.enter_context(tc.psum_pool(name="psum_x", bufs=1))
         psum_acc = stack.enter_context(tc.psum_pool(name="psum_acc", bufs=1))
+        psum_warm = stack.enter_context(tc.psum_pool(name="psum_warm", bufs=1))
 
         x_raw = keep.tile([P, C_QUARTER, PIXELS], BF16, align_bytes=256)
         nc.sync.dma_start(
@@ -75,11 +78,11 @@ def tile_locallyconnected2d_s_kernel(tc, x, weights, bias, out):
 
         x_sorted = keep.tile([P, WORDS, PIXELS, P_PIXEL, PAIR], BF16)
         x_t = psum_x.tile([P, WORDS, P], F32)
-        x_grouped = keep.tile([P, X_SLOTS, X_STRIDE, PACK], BF16, align_bytes=64)
-        x_codes = keep.tile([P, X_SLOTS * X_STRIDE], U32, align_bytes=64)
-        x_scales = keep.tile([P, X_SLOTS * X_STRIDE], U8, align_bytes=64)
+        x_grouped = keep.tile([P, QUARTERS, X_STRIDE, PACK], BF16, align_bytes=64)
+        zeros = keep.tile([P, ZERO_COLS, PACK], BF16, align_bytes=64)
+        x_codes = keep.tile([P, X_COLS + ZERO_COLS], U32, align_bytes=64)
+        x_scales = keep.tile([P, X_COLS + ZERO_COLS], U8, align_bytes=64)
 
-        nc.vector.memset(x_grouped[:].bitcast(F32), 0.0)
 
         def sort_x():
             by_s = x_raw[:].rearrange("r (p s e) q -> r s p e q", s=WORDS, e=PAIR)
@@ -97,19 +100,16 @@ def tile_locallyconnected2d_s_kernel(tc, x, weights, bias, out):
 
         def regroup_x():
             nc.scalar.copy(
-                out=x_grouped[:, :QUARTERS, :BATCH, :].bitcast(F32),
+                out=x_grouped[:, :, :BATCH, :].bitcast(F32),
                 in_=x_t[:].rearrange("p s (b k) -> p k b s", k=QUARTERS),
             )
 
-        def quantise_x():
-            values = x_grouped[:].rearrange("p k m t -> p (k m t)")
-            split = QUARTERS * X_STRIDE
-            for cols in (slice(0, split), slice(split, split + X_STRIDE)):
-                nc.vector.quantize_mx(
-                    out=x_codes[:, cols].bitcast(FP8X4),
-                    scales=x_scales[:, cols],
-                    in_=values[:, cols.start * PACK : cols.stop * PACK],
-                )
+        def quantise_columns(values, cols):
+            nc.vector.quantize_mx(
+                out=x_codes[:, cols].bitcast(FP8X4),
+                scales=x_scales[:, cols],
+                in_=values,
+            )
 
         w_codes = keep.tile([P, STEPS, OUT_CH], U32, align_bytes=64)
         w_scales = keep.tile([P, STEPS, OUT_CH], U8, align_bytes=64)
@@ -169,9 +169,29 @@ def tile_locallyconnected2d_s_kernel(tc, x, weights, bias, out):
                     stop=(k == QUARTERS - 1),
                 )
 
+        warm_sums = psum_warm.tile([P, ZERO_COLS], F32)
+
+        def warm(passes):
+            zero = slice(X_COLS, X_COLS + ZERO_COLS)
+            for n in range(passes):
+                nc.tensor.matmul_mx(
+                    out=warm_sums[:],
+                    lhsT=x_codes[:, X_COLS : X_COLS + P].bitcast(FP8X4),
+                    lhsT_scale=x_scales[:, X_COLS : X_COLS + P],
+                    rhs=x_codes[:, zero].bitcast(FP8X4),
+                    rhs_scale=x_scales[:, zero],
+                    start=True,
+                    stop=True,
+                )
+
         with tc.manual_schedule():
+            nc.vector.memset(zeros[:].bitcast(F32), 0.0)
+            quantise_columns(zeros[:].rearrange("p m t -> p (m t)"), slice(X_COLS, X_COLS + ZERO_COLS))
+            nc.vector.memset(x_grouped[:].bitcast(F32), 0.0)
+            warm(4)
             sort_x()
             transpose_x()
+            warm(2)
             regroup_x()
             for i in range(len(GROUPS) + MULTIPLY_LAG):
                 if i < len(GROUPS):
@@ -179,13 +199,15 @@ def tile_locallyconnected2d_s_kernel(tc, x, weights, bias, out):
                     transpose_taps(i)
                     regroup(i)
                 if i == 0:
-                    quantise_x()
+                    quantise_columns(x_grouped[:].rearrange("p k m t -> p (k m t)"), slice(0, X_COLS))
                 if 0 <= i - QUANTISE_LAG < len(GROUPS):
                     quantise(i - QUANTISE_LAG)
                 if i >= MULTIPLY_LAG:
                     loc, k = divmod(first_step[i - MULTIPLY_LAG] + GROUPS[i - MULTIPLY_LAG], QUARTERS)
                     if k == 0:
                         multiply(loc - 1)
+                if i < TAIL:
+                    warm(3 if i < TAIL - 1 else 2)
 
         result = keep.tile([BATCH, OUT_CH, LOCATIONS], F32)
         nc.vector.tensor_tensor(

@@ -200,14 +200,17 @@ def tile_locallyconnected2d_s_kernel(tc, x, weights, bias, out):
                     regroup(i)
                 if i == 0:
                     quantise_columns(x_grouped[:].rearrange("p k m t -> p (k m t)"), slice(0, X_COLS))
-                if 0 <= i - QUANTISE_LAG < len(GROUPS):
+                if QUANTISE_LAG <= i < TAIL:
                     quantise(i - QUANTISE_LAG)
+                elif i == len(GROUPS) - 1:
+                    for g in range(TAIL - QUANTISE_LAG, len(GROUPS)):
+                        quantise(g)
                 if i >= MULTIPLY_LAG:
                     loc, k = divmod(first_step[i - MULTIPLY_LAG] + GROUPS[i - MULTIPLY_LAG], QUARTERS)
                     if k == 0:
                         multiply(loc - 1)
-                if i < TAIL:
-                    warm(3 if i < TAIL - 1 else 2)
+                if i < TAIL - 1:
+                    warm(3)
 
         result = keep.tile([BATCH, OUT_CH, LOCATIONS], F32)
         nc.vector.tensor_tensor(

from contextlib import ExitStack

import concourse.mybir as mybir
from concourse.masks import make_identity

BF16 = mybir.dt.bfloat16
F32 = mybir.dt.float32
U32 = mybir.dt.uint32
U8 = mybir.dt.uint8
FP8X4 = mybir.dt.float8_e4m3fn_x4

P = 128
PACK = 4
PAIR = 2
WORDS = PACK // PAIR
BATCH = 32
CHANNELS = 512
OUT_CH = 128
SIDE = 2
TAPS = 3
PIXELS = SIDE * SIDE
LOCATIONS = SIDE * SIDE
QUARTERS = 4
P_PIXEL = P // PIXELS
C_QUARTER = CHANNELS // QUARTERS
STEPS = LOCATIONS * QUARTERS
GROUPS = (2,) * (STEPS // 2 - 1) + (1, 1)
X_STRIDE = 64
X_COLS = QUARTERS * X_STRIDE
ZERO_COLS = 256
TAIL = len(GROUPS) - 2
QUANTISE_LAG = 2
MULTIPLY_LAG = 3

FLOPS = 2 * BATCH * OUT_CH * LOCATIONS * PIXELS * CHANNELS
BYTES = (
    2 * BATCH * CHANNELS * PIXELS
    + 2 * LOCATIONS * OUT_CH * CHANNELS * PIXELS
    + 2 * OUT_CH * LOCATIONS
    + 4 * BATCH * OUT_CH * LOCATIONS
)


def tile_locallyconnected2d_s_kernel(tc, x, weights, bias, out):
    nc = tc.nc
    with ExitStack() as stack:
        w_pool = stack.enter_context(tc.tile_pool(name="w_pool", bufs=len(GROUPS)))
        keep = stack.enter_context(tc.tile_pool(name="keep", bufs=1))
        stage = stack.enter_context(tc.tile_pool(name="stage", bufs=4))
        psum_t = stack.enter_context(tc.psum_pool(name="psum_t", bufs=4))
        psum_x = stack.enter_context(tc.psum_pool(name="psum_x", bufs=1))
        psum_acc = stack.enter_context(tc.psum_pool(name="psum_acc", bufs=1))
        psum_warm = stack.enter_context(tc.psum_pool(name="psum_warm", bufs=1))

        x_raw = keep.tile([P, C_QUARTER, PIXELS], BF16, align_bytes=256)
        nc.sync.dma_start(
            out=x_raw[:], in_=x.rearrange("b (k c) y z -> (b k) c (y z)", k=QUARTERS)
        )
        bias_rows = keep.tile([BATCH, OUT_CH, LOCATIONS], BF16)
        w_rows = weights.rearrange("h w o c i j -> (h w) o c i j")
        w_raw = []
        first_step = []
        for steps in GROUPS:
            first_step.append(sum(GROUPS[: len(w_raw)]))
            loc, k = divmod(first_step[-1], QUARTERS)
            w_tile = w_pool.tile([P, steps * C_QUARTER, TAPS, TAPS], BF16, align_bytes=256, name="w_tile")
            nc.sync.dma_start(
                out=w_tile[:], in_=w_rows[loc, :, k * C_QUARTER : (k + steps) * C_QUARTER]
            )
            w_raw.append(w_tile)
        nc.sync.dma_start(
            out=bias_rows[:].rearrange("b o l -> b (o l)"),
            in_=bias.rearrange("o h w -> (o h w)").partition_broadcast(BATCH),
        )

        identity = keep.tile([P, P], F32)
        make_identity(nc, identity[:])

        x_sorted = keep.tile([P, WORDS, PIXELS, P_PIXEL, PAIR], BF16)
        x_t = psum_x.tile([P, WORDS, P], F32)
        x_grouped = keep.tile([P, QUARTERS, X_STRIDE, PACK], BF16, align_bytes=64)
        zeros = keep.tile([P, ZERO_COLS, PACK], BF16, align_bytes=64)
        x_codes = keep.tile([P, X_COLS + ZERO_COLS], U32, align_bytes=64)
        x_scales = keep.tile([P, X_COLS + ZERO_COLS], U8, align_bytes=64)


        def sort_x():
            by_s = x_raw[:].rearrange("r (p s e) q -> r s p e q", s=WORDS, e=PAIR)
            for s in range(WORDS):
                nc.vector.tensor_copy(
                    out=x_sorted[:, s].rearrange("r q p e -> r p e q"), in_=by_s[:, s]
                )

        def transpose_words(out, in_):
            nc.tensor.transpose(out, in_.rearrange("r q p e -> r (q p e)").bitcast(F32), identity[:])

        def transpose_x():
            for s in range(WORDS):
                transpose_words(x_t[:, s, :], x_sorted[:, s])

        def regroup_x():
            nc.scalar.copy(
                out=x_grouped[:, :, :BATCH, :].bitcast(F32),
                in_=x_t[:].rearrange("p s (b k) -> p k b s", k=QUARTERS),
            )

        def quantise_columns(values, cols):
            nc.vector.quantize_mx(
                out=x_codes[:, cols].bitcast(FP8X4),
                scales=x_scales[:, cols],
                in_=values,
            )

        w_codes = keep.tile([P, STEPS, OUT_CH], U32, align_bytes=64)
        w_scales = keep.tile([P, STEPS, OUT_CH], U8, align_bytes=64)
        acc = psum_acc.tile([P, LOCATIONS, OUT_CH], F32)
        w_sorted = {}
        w_t = {}
        w_grouped = {}

        def sort_taps(g):
            h, w = divmod(first_step[g] // QUARTERS, SIDE)
            taps = w_raw[g][:, :, 1 - h : 1 - h + SIDE, 1 - w : 1 - w + SIDE]
            by_s = taps.rearrange("o (n p s e) y z -> o s n p e y z", p=P_PIXEL, s=WORDS, e=PAIR)
            w_sorted[g] = stage.tile([P, GROUPS[g], WORDS, PIXELS, P_PIXEL, PAIR], BF16, name="w_sorted")
            by_channel = w_sorted[g][:].rearrange("o n s (y z) p e -> o s n p e y z", y=SIDE)
            for s in range(WORDS):
                nc.vector.tensor_copy(out=by_channel[:, s], in_=by_s[:, s])

        def transpose_taps(g):
            w_t[g] = psum_t.tile([P, GROUPS[g], WORDS, P], F32, name="w_t")
            for s in range(WORDS):
                for n in range(GROUPS[g]):
                    transpose_words(w_t[g][:, n, s, :], w_sorted[g][:, n, s])

        def o_parts(g):
            parts = 2 if g == len(GROUPS) - 1 else 1
            width = OUT_CH // parts
            return [slice(n * width, (n + 1) * width) for n in range(parts)]

        def regroup(g):
            w_grouped[g] = stage.tile([P, GROUPS[g], OUT_CH, PACK], BF16, align_bytes=64, name="w_grouped")
            for o_range in o_parts(g):
                nc.scalar.copy(
                    out=w_grouped[g][:, :, o_range].bitcast(F32),
                    in_=w_t[g][:, :, :, o_range].rearrange("p n s o -> p n o s"),
                )

        def quantise(g):
            steps = slice(first_step[g], first_step[g] + GROUPS[g])
            for o_range in o_parts(g):
                nc.vector.quantize_mx(
                    out=w_codes[:, steps, o_range].rearrange("p n o -> p (n o)").bitcast(FP8X4),
                    scales=w_scales[:, steps, o_range].rearrange("p n o -> p (n o)"),
                    in_=w_grouped[g][:, :, o_range].rearrange("p n o t -> p (n o t)"),
                )

        def multiply(loc):
            for k in range(QUARTERS):
                step = loc * QUARTERS + k
                x_cols = slice(k * X_STRIDE, k * X_STRIDE + P)
                nc.tensor.matmul_mx(
                    out=acc[:, loc, :],
                    lhsT=x_codes[:, x_cols].bitcast(FP8X4),
                    lhsT_scale=x_scales[:, x_cols],
                    rhs=w_codes[:, step, :].bitcast(FP8X4),
                    rhs_scale=w_scales[:, step, :],
                    start=(k == 0),
                    stop=(k == QUARTERS - 1),
                )

        warm_sums = psum_warm.tile([P, ZERO_COLS], F32)

        def warm(passes):
            zero = slice(X_COLS, X_COLS + ZERO_COLS)
            for n in range(passes):
                nc.tensor.matmul_mx(
                    out=warm_sums[:],
                    lhsT=x_codes[:, X_COLS : X_COLS + P].bitcast(FP8X4),
                    lhsT_scale=x_scales[:, X_COLS : X_COLS + P],
                    rhs=x_codes[:, zero].bitcast(FP8X4),
                    rhs_scale=x_scales[:, zero],
                    start=True,
                    stop=True,
                )

        with tc.manual_schedule():
            nc.vector.memset(zeros[:].bitcast(F32), 0.0)
            quantise_columns(zeros[:].rearrange("p m t -> p (m t)"), slice(X_COLS, X_COLS + ZERO_COLS))
            nc.vector.memset(x_grouped[:].bitcast(F32), 0.0)
            warm(4)
            sort_x()
            transpose_x()
            warm(2)
            regroup_x()
            for i in range(len(GROUPS) + MULTIPLY_LAG):
                if i < len(GROUPS):
                    sort_taps(i)
                    transpose_taps(i)
                    regroup(i)
                if i == 0:
                    quantise_columns(x_grouped[:].rearrange("p k m t -> p (k m t)"), slice(0, X_COLS))
                if QUANTISE_LAG <= i < TAIL:
                    quantise(i - QUANTISE_LAG)
                elif i == len(GROUPS) - 1:
                    for g in range(TAIL - QUANTISE_LAG, len(GROUPS)):
                        quantise(g)
                if i >= MULTIPLY_LAG:
                    loc, k = divmod(first_step[i - MULTIPLY_LAG] + GROUPS[i - MULTIPLY_LAG], QUARTERS)
                    if k == 0:
                        multiply(loc - 1)
                if i < TAIL - 1:
                    warm(3)

        result = keep.tile([BATCH, OUT_CH, LOCATIONS], F32)
        nc.vector.tensor_tensor(
            out=result[:],
            in0=acc[0:BATCH].rearrange("b l o -> b o l"),
            in1=bias_rows[:],
            op=mybir.AluOpType.add,
        )
        nc.sync.dma_start(
            out=out.rearrange("b o h w -> b (o h w)"),
            in_=result[:].rearrange("b o l -> b (o l)"),
        )
